import numpy as np
import ml_dtypes


def mxq(x, axis, fmt="e4m3"):
    dtype, down = {"e4m3": (ml_dtypes.float8_e4m3fn, 7), "e5m2": (ml_dtypes.float8_e5m2, 14)}[fmt]
    v = np.moveaxis(np.asarray(x, np.float32).astype(ml_dtypes.bfloat16).astype(np.float64), axis, -1)
    blocks = v.reshape(v.shape[:-1] + (-1, 32))
    amax = np.abs(blocks).max(-1, keepdims=True)
    byte = np.maximum(np.where(amax > 0, np.frexp(amax)[1] - 1 + 127, 0) - down, 1)
    scale = np.exp2(byte - 127.0)
    codes = (blocks / scale).astype(np.float32).astype(dtype).astype(np.float64)
    return np.moveaxis((codes * scale).reshape(v.shape), -1, axis)


WIDE = False


def mx_kscale(k):
    if not WIDE:
        return np.ones(k)
    levels = np.array([10, -10, 5, -5, 0])
    if k % 512:
        return np.exp2(np.random.permutation(np.resize(levels, k // 32))).repeat(32)
    a = np.empty((k // 512, 16))
    for p in range(k // 512):
        a[p, :8] = np.random.permutation(np.resize(levels, 8))
        for g in range(8):
            far = levels[np.abs(levels - a[p, g]) >= 10]
            a[p, g + 8] = far[np.random.randint(len(far))]
    return np.exp2(a.ravel()).repeat(32)


BF16 = ml_dtypes.bfloat16


def bf(x):
    return np.asarray(x, np.float32).astype(BF16)


def f64(x):
    return np.asarray(x).astype(np.float64)


B, S, HID, NH, HD, RD, RATIO = 4, 4096, 512, 2, 64, 32, 4
THETA = 10000.0
HALF = RD // 2


def rope_tables(positions):
    inv_freq = 1.0 / THETA ** (np.arange(HALF) / HALF)
    ang = positions[:, None] * inv_freq[None, :]
    return np.cos(ang), np.sin(ang)


def rope_interleaved(x, cos, sin):
    nope, rope = x[..., :-RD], x[..., -RD:]
    pr = rope.reshape(rope.shape[:-1] + (HALF, 2))
    a, b = pr[..., 0], pr[..., 1]
    new = np.stack([a * cos - b * sin, a * sin + b * cos], axis=-1).reshape(rope.shape)
    return np.concatenate([nope, new], axis=-1)


def setup_inputs():
    s = mx_kscale(HID)
    return {"hidden": bf(np.random.standard_normal((B, S, HID)) * s),
            "wq": bf(np.random.standard_normal((HID, NH * HD)) / np.sqrt(HID) / s[:, None])}


def reference(hidden, wq):
    q = mxq(f64(hidden), 2, "e4m3") @ mxq(f64(wq), 0, "e4m3")
    q = q.reshape(B, S, NH, HD).transpose(0, 2, 1, 3)
    cq, sq = rope_tables(np.arange(S))
    return rope_interleaved(q, cq, sq)

@@ -1,0 +1,294 @@
+import math
+from contextlib import ExitStack
+
+import concourse.mybir as mybir
+from concourse.masks import make_identity
+
+F32 = mybir.dt.float32
+BF16 = mybir.dt.bfloat16
+I32 = mybir.dt.int32
+U32 = mybir.dt.uint32
+U8 = mybir.dt.uint8
+FP8X4 = mybir.dt.float8_e4m3fn_x4
+ALU = mybir.AluOpType
+ACT = mybir.ActivationFunctionType
+
+P = 128
+BATCH, SEQ, HID = 4, 4096, 512
+HEADS, HEAD_DIM, ROPE_DIM = 2, 64, 32
+NOPE_DIM = HEAD_DIM - ROPE_DIM
+PAIRS = ROPE_DIM // 2
+FEATURES = HEADS * HEAD_DIM
+THETA = 10000.0
+FLOPS = 2 * BATCH * SEQ * HID * FEATURES
+
+WORDS = HID // 2
+TILES = SEQ // P
+GROUP = 4
+LOAD_TILES = 4
+STORE_TILES = 8
+N_GROUPS = BATCH * TILES // GROUP
+N_LOADS = BATCH * TILES // LOAD_TILES
+GROUPS_PER_LOAD = LOAD_TILES // GROUP
+LOADS_AHEAD = 32
+GROUPS_PER_STORE = STORE_TILES // GROUP
+GROUPS_PER_BATCH = TILES // GROUP
+ROTATED = GROUP * HEADS * PAIRS
+
+ROUND = 1.5 * 2.0**23
+COARSE = 2.0**14
+
+
+def tile_deepseekv4attention_pb_t_kernel(tc, hidden, wq, out):
+    nc = tc.nc
+    with ExitStack() as ctx:
+        const = ctx.enter_context(tc.tile_pool(name="const", bufs=1))
+        xpool = ctx.enter_context(tc.tile_pool(name="xpool", bufs=LOADS_AHEAD))
+        gpool = ctx.enter_context(tc.tile_pool(name="gpool", bufs=3))
+        qpool = ctx.enter_context(tc.tile_pool(name="qpool", bufs=3))
+        rpool = ctx.enter_context(tc.tile_pool(name="rpool", bufs=2))
+        spool = ctx.enter_context(tc.tile_pool(name="spool", bufs=12))
+        tpsum = ctx.enter_context(tc.psum_pool(name="tpsum", bufs=4))
+        ypsum = ctx.enter_context(tc.psum_pool(name="ypsum", bufs=4))
+        ctx.enter_context(tc.manual_schedule())
+
+        w_raw = const.tile([P, 4, FEATURES], BF16)
+        nc.scalar.dma_start(out=w_raw[:], in_=wq.rearrange("(p t) n -> p t n", t=4))
+        x_of = {}
+
+        def load_tiles(load):
+            b, first = divmod(load * LOAD_TILES, TILES)
+            x_sb = xpool.tile([P, LOAD_TILES * HID], BF16)
+            nc.sync.dma_start(
+                out=x_sb[:],
+                in_=hidden[b].rearrange("(p c) k -> p (c k)", c=TILES)[
+                    :, first * HID : (first + LOAD_TILES) * HID
+                ],
+            )
+            x_of[load] = x_sb
+
+        for load in range(LOADS_AHEAD):
+            load_tiles(load)
+
+        position_i = const.tile([P, TILES], I32)
+        nc.gpsimd.iota(position_i[:], pattern=[[1, TILES]], base=0, channel_multiplier=TILES)
+        ident = const.tile([P, P], F32)
+        make_identity(nc, ident[:])
+
+        zero = const.tile([P, 1], F32)
+        nc.vector.memset(zero[:], 0.0)
+        warm = const.tile([P, 1], F32)
+        nc.scalar.activation(out=warm[:], in_=zero[:], func=ACT.Sin)
+
+        position = const.tile([P, TILES], F32)
+        nc.vector.tensor_copy(out=position[:], in_=position_i[:])
+        coarse = const.tile([P, TILES, PAIRS], F32)
+        fine = const.tile([P, TILES, PAIRS], F32)
+        for j in range(PAIRS):
+            turns = THETA ** (-j / PAIRS) / (2.0 * math.pi)
+            turns_coarse = round(turns * COARSE) / COARSE
+            nc.vector.tensor_scalar(
+                out=coarse[:, :, j : j + 1],
+                in0=position[:].unsqueeze(2),
+                scalar1=turns_coarse,
+                scalar2=None,
+                op0=ALU.mult,
+            )
+            nc.scalar.mul(
+                out=fine[:, :, j : j + 1], in_=position[:].unsqueeze(2), mul=turns - turns_coarse
+            )
+        whole = const.tile([P, TILES, PAIRS], F32)
+        nc.vector.tensor_scalar(
+            out=whole[:], in0=coarse[:], scalar1=ROUND, scalar2=ROUND, op0=ALU.add, op1=ALU.subtract
+        )
+        part = const.tile([P, TILES, PAIRS], F32)
+        nc.vector.tensor_tensor(out=part[:], in0=coarse[:], in1=whole[:], op=ALU.subtract)
+        both = const.tile([P, TILES, PAIRS], F32)
+        nc.vector.tensor_tensor(out=both[:], in0=part[:], in1=fine[:], op=ALU.add)
+        whole2 = const.tile([P, TILES, PAIRS], F32)
+        nc.vector.tensor_scalar(
+            out=whole2[:], in0=both[:], scalar1=ROUND, scalar2=ROUND, op0=ALU.add, op1=ALU.subtract
+        )
+        turn = const.tile([P, TILES, PAIRS], F32)
+        nc.vector.tensor_tensor(out=turn[:], in0=both[:], in1=whole2[:], op=ALU.subtract)
+        size = const.tile([P, TILES, PAIRS], F32)
+        nc.vector.scalar_tensor_tensor(
+            out=size[:], in0=turn[:], scalar=-1.0, in1=turn[:], op0=ALU.mult, op1=ALU.max
+        )
+        quarter = const.tile([P, TILES, PAIRS], F32)
+        nc.vector.tensor_scalar(
+            out=quarter[:], in0=size[:], scalar1=-1.0, scalar2=0.25, op0=ALU.mult, op1=ALU.add
+        )
+        cos_t = const.tile([P, TILES, HEADS, PAIRS], F32)
+        sin_t = const.tile([P, TILES, HEADS, PAIRS], F32)
+        nsin_t = const.tile([P, TILES, HEADS, PAIRS], F32)
+
+        def fill_tables(g):
+            tiles = slice(g * GROUP, (g + 1) * GROUP)
+            shape = [P, GROUP, HEADS, PAIRS]
+            for table, turns_of, scale in (
+                (cos_t, quarter, 2.0 * math.pi),
+                (sin_t, turn, 2.0 * math.pi),
+                (nsin_t, turn, -2.0 * math.pi),
+            ):
+                nc.scalar.activation(
+                    out=table[:, tiles],
+                    in_=turns_of[:, tiles].unsqueeze(2).to_broadcast(shape),
+                    func=ACT.Sin,
+                    scale=scale,
+                )
+
+        w_grouped = const.tile([P, FEATURES, 4], BF16, align_bytes=64)
+        by_head = w_raw[:].rearrange("p t (h d) -> p h d t", h=HEADS)
+        nc.vector.tensor_copy(
+            out=w_grouped[:, 0 : HEADS * NOPE_DIM, :].rearrange("p (h d) t -> p h d t", h=HEADS),
+            in_=by_head[:, :, 0:NOPE_DIM, :],
+        )
+        by_pair = by_head[:, :, NOPE_DIM:HEAD_DIM, :].rearrange("p h (j e) t -> p e h j t", e=2)
+        for e in range(2):
+            first = HEADS * (NOPE_DIM + e * PAIRS)
+            nc.vector.tensor_copy(
+                out=w_grouped[:, first : first + HEADS * PAIRS, :].rearrange(
+                    "p (h j) t -> p h j t", h=HEADS
+                ),
+                in_=by_pair[:, e],
+            )
+        w_codes = const.tile([P, FEATURES], U32, align_bytes=64)
+        w_scales = const.tile([P, FEATURES], U8, align_bytes=64)
+        nc.vector.quantize_mx(
+            out=w_codes[:].bitcast(FP8X4),
+            scales=w_scales[:],
+            in_=w_grouped[:].rearrange("p n t -> p (n t)"),
+        )
+
+        xt_of, grouped_of, codes_of, scales_of, y_of, stage_of, products_of = {}, {}, {}, {}, {}, {}, {}
+
+        def transpose_group(g):
+            x_words = x_of[g // GROUPS_PER_LOAD][:].bitcast(F32)
+            first = (g % GROUPS_PER_LOAD) * GROUP * WORDS
+            banks = []
+            for half in range(2):
+                xt = tpsum.tile([P, 2, 2, P], F32)
+                for i in range(2):
+                    for u in range(2):
+                        start = first + (2 * half + i) * WORDS
+                        nc.tensor.transpose(
+                            xt[:, i, u, :], x_words[:, start + u : start + WORDS : 2], ident[:]
+                        )
+                banks.append(xt)
+            xt_of[g] = banks
+
+        def regroup_group(g):
+            grouped = gpool.tile([P, GROUP * HID], BF16, align_bytes=64)
+            grouped_words = grouped[:].bitcast(F32).rearrange(
+                "p (half i r u) -> p half i r u", half=2, i=2, u=2
+            )
+            for half in range(2):
+                nc.scalar.copy(
+                    out=grouped_words[:, half],
+                    in_=xt_of[g][half][:].rearrange("p i u r -> p i r u"),
+                )
+            grouped_of[g] = grouped
+
+        def quantise_group(g):
+            codes = qpool.tile([P, GROUP * P], U32, align_bytes=64)
+            scales = qpool.tile([P, GROUP * P], U8, align_bytes=64)
+            nc.vector.quantize_mx(
+                out=codes[:].bitcast(FP8X4), scales=scales[:], in_=grouped_of[g][:]
+            )
+            codes_of[g] = codes
+            scales_of[g] = scales
+
+        def multiply_group(g):
+            y = ypsum.tile([P, GROUP, FEATURES], F32)
+            for i in range(GROUP):
+                tokens = slice(i * P, (i + 1) * P)
+                nc.tensor.matmul_mx(
+                    out=y[:, i, :],
+                    lhsT=codes_of[g][:, tokens].bitcast(FP8X4),
+                    lhsT_scale=scales_of[g][:, tokens],
+                    rhs=w_codes[:].bitcast(FP8X4),
+                    rhs_scale=w_scales[:],
+                    start=True,
+                    stop=True,
+                )
+            y_of[g] = y
+
+        def stage_part(g, features):
+            first = (g % GROUPS_PER_STORE) * GROUP
+            return stage_of[g // GROUPS_PER_STORE][:, :, first : first + GROUP, features]
+
+        def copy_unrotated(g):
+            if g % GROUPS_PER_STORE == 0:
+                stage = spool.tile([P, HEADS, STORE_TILES, HEAD_DIM], F32)
+                stage_of[g // GROUPS_PER_STORE] = stage
+            nc.scalar.copy(
+                out=stage_part(g, slice(0, NOPE_DIM)).rearrange("p h c d -> p c h d"),
+                in_=y_of[g][:, :, 0 : HEADS * NOPE_DIM].rearrange("p c (h d) -> p c h d", h=HEADS),
+            )
+
+        def rotate_products(g):
+            tiles = slice((g % GROUPS_PER_BATCH) * GROUP, (g % GROUPS_PER_BATCH + 1) * GROUP)
+            pair_halves = y_of[g][:, :, HEADS * NOPE_DIM : FEATURES].rearrange(
+                "p c (e x) -> p e c x", e=2
+            )
+            by_cos = rpool.tile([P, 2, ROTATED], F32)
+            by_sin = rpool.tile([P, 2, ROTATED], F32)
+            nc.vector.tensor_tensor(
+                out=by_cos[:].rearrange("p e (c x) -> p e c x", c=GROUP),
+                in0=pair_halves,
+                in1=cos_t[:, tiles]
+                .rearrange("p c h j -> p c (h j)")
+                .unsqueeze(1)
+                .to_broadcast([P, 2, GROUP, HEADS * PAIRS]),
+                op=ALU.mult,
+            )
+            for e, table in ((0, nsin_t), (1, sin_t)):
+                nc.vector.tensor_tensor(
+                    out=by_sin[:, e, :].rearrange("p (c x) -> p c x", c=GROUP),
+                    in0=pair_halves[:, 1 - e],
+                    in1=table[:, tiles].rearrange("p c h j -> p c (h j)"),
+                    op=ALU.mult,
+                )
+            products_of[g] = (by_cos, by_sin)
+
+        def rotate_sum(g):
+            by_cos, by_sin = products_of[g]
+            order = "p e (c h j) -> p c h j e"
+            nc.vector.tensor_tensor(
+                out=stage_part(g, slice(NOPE_DIM, HEAD_DIM)).rearrange(
+                    "p h c (j e) -> p c h j e", e=2
+                ),
+                in0=by_cos[:].rearrange(order, c=GROUP, h=HEADS),
+                in1=by_sin[:].rearrange(order, c=GROUP, h=HEADS),
+                op=ALU.add,
+            )
+
+        def store_group(g):
+            if g % GROUPS_PER_STORE == GROUPS_PER_STORE - 1:
+                b, first = divmod((g + 1) * GROUP - STORE_TILES, TILES)
+                nc.sync.dma_start(
+                    out=out[b].rearrange("h (p c) d -> p h c d", c=TILES)[
+                        :, :, first : first + STORE_TILES, :
+                    ],
+                    in_=stage_of[g // GROUPS_PER_STORE][:],
+                )
+
+        for step in range(N_GROUPS + 3):
+            if step < N_GROUPS:
+                transpose_group(step)
+                regroup_group(step)
+            if step + LOADS_AHEAD < N_LOADS:
+                load_tiles(step + LOADS_AHEAD)
+            if step < GROUPS_PER_BATCH:
+                fill_tables(step)
+            if step >= 3:
+                rotate_products(step - 3)
+            if 1 <= step <= N_GROUPS:
+                quantise_group(step - 1)
+            if 2 <= step <= N_GROUPS + 1:
+                multiply_group(step - 2)
+                copy_unrotated(step - 2)
+            if step >= 3:
+                rotate_sum(step - 3)
+                store_group(step - 3)

@@ -6,7 +6,6 @@ from concourse.masks import make_identity
 
 F32 = mybir.dt.float32
 BF16 = mybir.dt.bfloat16
-I32 = mybir.dt.int32
 U32 = mybir.dt.uint32
 U8 = mybir.dt.uint8
 FP8X4 = mybir.dt.float8_e4m3fn_x4
@@ -24,16 +23,17 @@ FLOPS = 2 * BATCH * SEQ * HID * FEATURES
 
 WORDS = HID // 2
 TILES = SEQ // P
+ALL_TILES = BATCH * TILES
 GROUP = 4
-LOAD_TILES = 4
-STORE_TILES = 8
-N_GROUPS = BATCH * TILES // GROUP
-N_LOADS = BATCH * TILES // LOAD_TILES
-GROUPS_PER_LOAD = LOAD_TILES // GROUP
-LOADS_AHEAD = 32
-GROUPS_PER_STORE = STORE_TILES // GROUP
-GROUPS_PER_BATCH = TILES // GROUP
-ROTATED = GROUP * HEADS * PAIRS
+N_GROUPS = ALL_TILES // GROUP
+STORE_GROUPS = 2
+STORE_TILES = STORE_GROUPS * GROUP
+LOADS = [1, 1, 2] + [4] * 5 + [8] * 13
+LOAD_TILES = max(LOADS)
+RUNS = [1] * 4 + [2] * 12 + [1] * 4
+
+X_BUFS = 9
+CHUNKS = 4
 
 ROUND = 1.5 * 2.0**23
 COARSE = 2.0**14
@@ -43,35 +43,47 @@ def tile_deepseekv4attention_pb_t_kernel(tc, hidden, wq, out):
     nc = tc.nc
     with ExitStack() as ctx:
         const = ctx.enter_context(tc.tile_pool(name="const", bufs=1))
-        xpool = ctx.enter_context(tc.tile_pool(name="xpool", bufs=LOADS_AHEAD))
+        xpool = ctx.enter_context(tc.tile_pool(name="xpool", bufs=X_BUFS))
+        hpool = ctx.enter_context(tc.tile_pool(name="hpool", bufs=2))
         gpool = ctx.enter_context(tc.tile_pool(name="gpool", bufs=3))
         qpool = ctx.enter_context(tc.tile_pool(name="qpool", bufs=3))
         rpool = ctx.enter_context(tc.tile_pool(name="rpool", bufs=2))
-        spool = ctx.enter_context(tc.tile_pool(name="spool", bufs=12))
+        spool = ctx.enter_context(tc.tile_pool(name="spool", bufs=14))
         tpsum = ctx.enter_context(tc.psum_pool(name="tpsum", bufs=4))
         ypsum = ctx.enter_context(tc.psum_pool(name="ypsum", bufs=4))
         ctx.enter_context(tc.manual_schedule())
 
-        w_raw = const.tile([P, 4, FEATURES], BF16)
-        nc.scalar.dma_start(out=w_raw[:], in_=wq.rearrange("(p t) n -> p t n", t=4))
         x_of = {}
 
-        def load_tiles(load):
-            b, first = divmod(load * LOAD_TILES, TILES)
-            x_sb = xpool.tile([P, LOAD_TILES * HID], BF16)
+        def load_tiles(n):
+            size, first = LOADS[n], sum(LOADS[:n])
+            b, c = divmod(first, TILES)
+            if size == LOAD_TILES:
+                x_sb = xpool.tile([P, size * HID], BF16)
+            else:
+                x_sb = const.tile([P, size * HID], BF16, name="x%d" % n)
             nc.sync.dma_start(
                 out=x_sb[:],
-                in_=hidden[b].rearrange("(p c) k -> p (c k)", c=TILES)[
-                    :, first * HID : (first + LOAD_TILES) * HID
-                ],
+                in_=hidden[b].rearrange("(p c) k -> p (c k)", c=TILES)[:, c * HID : (c + size) * HID],
             )
-            x_of[load] = x_sb
+            for i in range(size):
+                x_of[first + i] = (x_sb, i)
 
-        for load in range(LOADS_AHEAD):
-            load_tiles(load)
+        loads_ahead = LOADS.index(LOAD_TILES) + X_BUFS
+        for n in range(loads_ahead):
+            load_tiles(n)
 
-        position_i = const.tile([P, TILES], I32)
-        nc.gpsimd.iota(position_i[:], pattern=[[1, TILES]], base=0, channel_multiplier=TILES)
+        w_raw = const.tile([P, 4, FEATURES], BF16)
+        nc.scalar.dma_start(out=w_raw[:], in_=wq.rearrange("(p t) n -> p t n", t=4))
+
+        position = const.tile([P, TILES], F32)
+        nc.gpsimd.iota(
+            position[:],
+            pattern=[[1, TILES]],
+            base=0,
+            channel_multiplier=TILES,
+            allow_small_or_imprecise_dtypes=True,
+        )
         ident = const.tile([P, P], F32)
         make_identity(nc, ident[:])
 
@@ -80,78 +92,96 @@ def tile_deepseekv4attention_pb_t_kernel(tc, hidden, wq, out):
         warm = const.tile([P, 1], F32)
         nc.scalar.activation(out=warm[:], in_=zero[:], func=ACT.Sin)
 
-        position = const.tile([P, TILES], F32)
-        nc.vector.tensor_copy(out=position[:], in_=position_i[:])
-        coarse = const.tile([P, TILES, PAIRS], F32)
-        fine = const.tile([P, TILES, PAIRS], F32)
-        for j in range(PAIRS):
+        coarse = const.tile([P, PAIRS, TILES], F32)
+        fine = const.tile([P, PAIRS, TILES], F32)
+
+        def frequency(j):
             turns = THETA ** (-j / PAIRS) / (2.0 * math.pi)
             turns_coarse = round(turns * COARSE) / COARSE
-            nc.vector.tensor_scalar(
-                out=coarse[:, :, j : j + 1],
-                in0=position[:].unsqueeze(2),
-                scalar1=turns_coarse,
-                scalar2=None,
-                op0=ALU.mult,
-            )
-            nc.scalar.mul(
-                out=fine[:, :, j : j + 1], in_=position[:].unsqueeze(2), mul=turns - turns_coarse
-            )
-        whole = const.tile([P, TILES, PAIRS], F32)
-        nc.vector.tensor_scalar(
-            out=whole[:], in0=coarse[:], scalar1=ROUND, scalar2=ROUND, op0=ALU.add, op1=ALU.subtract
-        )
-        part = const.tile([P, TILES, PAIRS], F32)
-        nc.vector.tensor_tensor(out=part[:], in0=coarse[:], in1=whole[:], op=ALU.subtract)
-        both = const.tile([P, TILES, PAIRS], F32)
-        nc.vector.tensor_tensor(out=both[:], in0=part[:], in1=fine[:], op=ALU.add)
-        whole2 = const.tile([P, TILES, PAIRS], F32)
-        nc.vector.tensor_scalar(
-            out=whole2[:], in0=both[:], scalar1=ROUND, scalar2=ROUND, op0=ALU.add, op1=ALU.subtract
-        )
-        turn = const.tile([P, TILES, PAIRS], F32)
-        nc.vector.tensor_tensor(out=turn[:], in0=both[:], in1=whole2[:], op=ALU.subtract)
-        size = const.tile([P, TILES, PAIRS], F32)
-        nc.vector.scalar_tensor_tensor(
-            out=size[:], in0=turn[:], scalar=-1.0, in1=turn[:], op0=ALU.mult, op1=ALU.max
-        )
-        quarter = const.tile([P, TILES, PAIRS], F32)
-        nc.vector.tensor_scalar(
-            out=quarter[:], in0=size[:], scalar1=-1.0, scalar2=0.25, op0=ALU.mult, op1=ALU.add
-        )
-        cos_t = const.tile([P, TILES, HEADS, PAIRS], F32)
-        sin_t = const.tile([P, TILES, HEADS, PAIRS], F32)
-        nsin_t = const.tile([P, TILES, HEADS, PAIRS], F32)
+            return turns_coarse, turns - turns_coarse
 
-        def fill_tables(g):
-            tiles = slice(g * GROUP, (g + 1) * GROUP)
-            shape = [P, GROUP, HEADS, PAIRS]
-            for table, turns_of, scale in (
-                (cos_t, quarter, 2.0 * math.pi),
-                (sin_t, turn, 2.0 * math.pi),
-                (nsin_t, turn, -2.0 * math.pi),
-            ):
-                nc.scalar.activation(
-                    out=table[:, tiles],
-                    in_=turns_of[:, tiles].unsqueeze(2).to_broadcast(shape),
-                    func=ACT.Sin,
-                    scale=scale,
-                )
+        def scale_position(engine, angle, j, factor):
+            engine.tensor_scalar(
+                out=angle[:, j, :],
+                in0=position[:],
+                scalar1=factor,
+                scalar2=0.0,
+                op0=ALU.mult,
+                op1=ALU.add,
+            )
+
+        for j in range(PAIRS):
+            scale_position(nc.vector, coarse, j, frequency(j)[0])
+        for j in range(0, 4):
+            nc.scalar.mul(out=fine[:, j, :], in_=position[:], mul=frequency(j)[1])
+        for j in range(4, 10):
+            scale_position(nc.gpsimd, fine, j, frequency(j)[1])
+        for j in range(10, PAIRS):
+            scale_position(nc.vector, fine, j, frequency(j)[1])
+        whole = const.tile([P, PAIRS, TILES], F32)
+        part = const.tile([P, PAIRS, TILES], F32)
+        both = const.tile([P, PAIRS, TILES], F32)
+        whole2 = const.tile([P, PAIRS, TILES], F32)
+        turn = const.tile([P, PAIRS, TILES], F32)
+        tables = const.tile([P, TILES, 2, 2, PAIRS], F32)
+
+        def round_angles(rounded, angles, tiles):
+            nc.vector.tensor_scalar(
+                out=rounded[:, :, tiles],
+                in0=angles[:, :, tiles],
+                scalar1=ROUND,
+                scalar2=ROUND,
+                op0=ALU.add,
+                op1=ALU.subtract,
+            )
+
+        def combine_angles(engine, result, a, b, op, tiles):
+            engine.tensor_tensor(
+                out=result[:, :, tiles], in0=a[:, :, tiles], in1=b[:, :, tiles], op=op
+            )
+
+        def fill_tables(engine, tiles):
+            n = tiles.stop - tiles.start
+            half = hpool.tile([P, n, PAIRS], F32)
+            square = hpool.tile([P, n, PAIRS], F32)
+            turns = turn[:, :, tiles].rearrange("p j c -> p c j")
+            nc.scalar.activation(out=half[:], in_=turns, func=ACT.Sin, scale=math.pi)
+            nc.scalar.activation(
+                out=tables[:, tiles, 0, 1, :], in_=turns, func=ACT.Sin, scale=2.0 * math.pi
+            )
+            nc.scalar.activation(
+                out=tables[:, tiles, 1, 0, :], in_=turns, func=ACT.Sin, scale=-2.0 * math.pi
+            )
+            engine.tensor_tensor(out=square[:], in0=half[:], in1=half[:], op=ALU.mult)
+            engine.tensor_scalar(
+                out=tables[:, tiles].rearrange("p c i e j -> p c (i e) j")[:, :, 0:4:3, :],
+                in0=square[:].unsqueeze(2).to_broadcast([P, n, 2, PAIRS]),
+                scalar1=-2.0,
+                scalar2=1.0,
+                op0=ALU.mult,
+                op1=ALU.add,
+            )
+
+        def chunk_of(key):
+            return slice(key * TILES // CHUNKS, (key + 1) * TILES // CHUNKS)
+
+        first_chunk, other_chunks = chunk_of(0), slice(TILES // CHUNKS, TILES)
+        round_angles(whole, coarse, slice(0, TILES))
+        combine_angles(nc.gpsimd, part, coarse, whole, ALU.subtract, other_chunks)
+        combine_angles(nc.gpsimd, both, part, fine, ALU.add, other_chunks)
+        combine_angles(nc.vector, part, coarse, whole, ALU.subtract, first_chunk)
+        combine_angles(nc.vector, both, part, fine, ALU.add, first_chunk)
+        round_angles(whole2, both, first_chunk)
+        combine_angles(nc.vector, turn, both, whole2, ALU.subtract, first_chunk)
 
         w_grouped = const.tile([P, FEATURES, 4], BF16, align_bytes=64)
+        w_parts = w_grouped[:].rearrange("p (i s n) t -> p i s n t", i=2, s=2)
         by_head = w_raw[:].rearrange("p t (h d) -> p h d t", h=HEADS)
-        nc.vector.tensor_copy(
-            out=w_grouped[:, 0 : HEADS * NOPE_DIM, :].rearrange("p (h d) t -> p h d t", h=HEADS),
-            in_=by_head[:, :, 0:NOPE_DIM, :],
-        )
+        nc.scalar.copy(out=w_parts[:, :, 1], in_=by_head[:, :, 0:NOPE_DIM, :])
         by_pair = by_head[:, :, NOPE_DIM:HEAD_DIM, :].rearrange("p h (j e) t -> p e h j t", e=2)
         for e in range(2):
-            first = HEADS * (NOPE_DIM + e * PAIRS)
             nc.vector.tensor_copy(
-                out=w_grouped[:, first : first + HEADS * PAIRS, :].rearrange(
-                    "p (h j) t -> p h j t", h=HEADS
-                ),
-                in_=by_pair[:, e],
+                out=w_parts[:, e, 0].rearrange("p (h j) t -> p h j t", h=HEADS), in_=by_pair[:, e]
             )
         w_codes = const.tile([P, FEATURES], U32, align_bytes=64)
         w_scales = const.tile([P, FEATURES], U8, align_bytes=64)
@@ -163,132 +193,148 @@ def tile_deepseekv4attention_pb_t_kernel(tc, hidden, wq, out):
 
         xt_of, grouped_of, codes_of, scales_of, y_of, stage_of, products_of = {}, {}, {}, {}, {}, {}, {}
 
-        def transpose_group(g):
-            x_words = x_of[g // GROUPS_PER_LOAD][:].bitcast(F32)
-            first = (g % GROUPS_PER_LOAD) * GROUP * WORDS
-            banks = []
-            for half in range(2):
-                xt = tpsum.tile([P, 2, 2, P], F32)
-                for i in range(2):
-                    for u in range(2):
-                        start = first + (2 * half + i) * WORDS
-                        nc.tensor.transpose(
-                            xt[:, i, u, :], x_words[:, start + u : start + WORDS : 2], ident[:]
-                        )
-                banks.append(xt)
-            xt_of[g] = banks
+        def transpose_run(run):
+            for g in run:
+                for half in range(2):
+                    xt = tpsum.tile([P, 2, 2, P], F32)
+                    for i in range(2):
+                        x_sb, place = x_of[g * GROUP + 2 * half + i]
+                        x_words = x_sb[:].bitcast(F32)
+                        for u in range(2):
+                            nc.tensor.transpose(
+                                xt[:, i, u, :],
+                                x_words[:, place * WORDS + u : (place + 1) * WORDS : 2],
+                                ident[:],
+                            )
+                    xt_of[g, half] = xt
 
-        def regroup_group(g):
-            grouped = gpool.tile([P, GROUP * HID], BF16, align_bytes=64)
+        def regroup_run(run):
+            grouped = gpool.tile([P, len(run) * GROUP * HID], BF16, align_bytes=64)
             grouped_words = grouped[:].bitcast(F32).rearrange(
-                "p (half i r u) -> p half i r u", half=2, i=2, u=2
+                "p (half i r u) -> p half i r u", i=2, r=P, u=2
             )
-            for half in range(2):
-                nc.scalar.copy(
-                    out=grouped_words[:, half],
-                    in_=xt_of[g][half][:].rearrange("p i u r -> p i r u"),
-                )
-            grouped_of[g] = grouped
+            for n, g in enumerate(run):
+                for half in range(2):
+                    nc.scalar.copy(
+                        out=grouped_words[:, 2 * n + half],
+                        in_=xt_of[g, half][:].rearrange("p i u r -> p i r u"),
+                    )
+            grouped_of[run[0]] = grouped
 
-        def quantise_group(g):
-            codes = qpool.tile([P, GROUP * P], U32, align_bytes=64)
-            scales = qpool.tile([P, GROUP * P], U8, align_bytes=64)
+        def quantise_run(run):
+            codes = qpool.tile([P, len(run) * GROUP * P], U32, align_bytes=64)
+            scales = qpool.tile([P, len(run) * GROUP * P], U8, align_bytes=64)
             nc.vector.quantize_mx(
-                out=codes[:].bitcast(FP8X4), scales=scales[:], in_=grouped_of[g][:]
+                out=codes[:].bitcast(FP8X4), scales=scales[:], in_=grouped_of[run[0]][:]
             )
-            codes_of[g] = codes
-            scales_of[g] = scales
+            codes_of[run[0]] = codes
+            scales_of[run[0]] = scales
 
-        def multiply_group(g):
-            y = ypsum.tile([P, GROUP, FEATURES], F32)
-            for i in range(GROUP):
-                tokens = slice(i * P, (i + 1) * P)
-                nc.tensor.matmul_mx(
-                    out=y[:, i, :],
-                    lhsT=codes_of[g][:, tokens].bitcast(FP8X4),
-                    lhsT_scale=scales_of[g][:, tokens],
-                    rhs=w_codes[:].bitcast(FP8X4),
-                    rhs_scale=w_scales[:],
-                    start=True,
-                    stop=True,
-                )
-            y_of[g] = y
+        def multiply_run(run):
+            codes, scales = codes_of[run[0]], scales_of[run[0]]
+            for n, g in enumerate(run):
+                y = ypsum.tile([P, GROUP, FEATURES], F32)
+                for i in range(GROUP):
+                    tokens = slice((n * GROUP + i) * P, (n * GROUP + i + 1) * P)
+                    nc.tensor.matmul_mx(
+                        out=y[:, i, :],
+                        lhsT=codes[:, tokens].bitcast(FP8X4),
+                        lhsT_scale=scales[:, tokens],
+                        rhs=w_codes[:].bitcast(FP8X4),
+                        rhs_scale=w_scales[:],
+                        start=True,
+                        stop=True,
+                    )
+                y_of[g] = y
 
-        def stage_part(g, features):
-            first = (g % GROUPS_PER_STORE) * GROUP
-            return stage_of[g // GROUPS_PER_STORE][:, :, first : first + GROUP, features]
+        def stage_part(run, features):
+            first = (run[0] % STORE_GROUPS) * GROUP
+            tiles = slice(first, first + len(run) * GROUP)
+            return stage_of[run[0] // STORE_GROUPS][:, :, tiles, features]
 
-        def copy_unrotated(g):
-            if g % GROUPS_PER_STORE == 0:
+        def copy_unrotated(run):
+            if run[0] % STORE_GROUPS == 0:
                 stage = spool.tile([P, HEADS, STORE_TILES, HEAD_DIM], F32)
-                stage_of[g // GROUPS_PER_STORE] = stage
-            nc.scalar.copy(
-                out=stage_part(g, slice(0, NOPE_DIM)).rearrange("p h c d -> p c h d"),
-                in_=y_of[g][:, :, 0 : HEADS * NOPE_DIM].rearrange("p c (h d) -> p c h d", h=HEADS),
-            )
+                stage_of[run[0] // STORE_GROUPS] = stage
+            for g in run:
+                nc.scalar.copy(
+                    out=stage_part([g], slice(0, NOPE_DIM)).rearrange("p h c d -> p c h d"),
+                    in_=y_of[g][:].rearrange("p c (h s d) -> p c h s d", h=HEADS, s=2)[:, :, :, 1],
+                )
 
-        def rotate_products(g):
-            tiles = slice((g % GROUPS_PER_BATCH) * GROUP, (g % GROUPS_PER_BATCH + 1) * GROUP)
-            pair_halves = y_of[g][:, :, HEADS * NOPE_DIM : FEATURES].rearrange(
-                "p c (e x) -> p e c x", e=2
-            )
-            by_cos = rpool.tile([P, 2, ROTATED], F32)
-            by_sin = rpool.tile([P, 2, ROTATED], F32)
-            nc.vector.tensor_tensor(
-                out=by_cos[:].rearrange("p e (c x) -> p e c x", c=GROUP),
-                in0=pair_halves,
-                in1=cos_t[:, tiles]
-                .rearrange("p c h j -> p c (h j)")
-                .unsqueeze(1)
-                .to_broadcast([P, 2, GROUP, HEADS * PAIRS]),
-                op=ALU.mult,
-            )
-            for e, table in ((0, nsin_t), (1, sin_t)):
+        def rotate_products(run):
+            products = rpool.tile([P, len(run), GROUP * 2, 2, HEADS, PAIRS], F32)
+            shape = [P, GROUP * 2, 2, HEADS, PAIRS]
+            for n, g in enumerate(run):
+                first = g * GROUP % TILES
                 nc.vector.tensor_tensor(
-                    out=by_sin[:, e, :].rearrange("p (c x) -> p c x", c=GROUP),
-                    in0=pair_halves[:, 1 - e],
-                    in1=table[:, tiles].rearrange("p c h j -> p c (h j)"),
+                    out=products[:, n],
+                    in0=y_of[g][:]
+                    .rearrange("p c (i s h j) -> p (c i) s h j", i=2, s=2, h=HEADS)[:, :, 0:1]
+                    .to_broadcast(shape),
+                    in1=tables[:, first : first + GROUP]
+                    .rearrange("p c i e j -> p (c i) e j")
+                    .unsqueeze(3)
+                    .to_broadcast(shape),
                     op=ALU.mult,
                 )
-            products_of[g] = (by_cos, by_sin)
+            products_of[run[0]] = products
 
-        def rotate_sum(g):
-            by_cos, by_sin = products_of[g]
-            order = "p e (c h j) -> p c h j e"
+        def rotate_sum(run):
+            terms = products_of[run[0]][:].rearrange("p n (c i) e h j -> p i (n c) h j e", i=2)
             nc.vector.tensor_tensor(
-                out=stage_part(g, slice(NOPE_DIM, HEAD_DIM)).rearrange(
+                out=stage_part(run, slice(NOPE_DIM, HEAD_DIM)).rearrange(
                     "p h c (j e) -> p c h j e", e=2
                 ),
-                in0=by_cos[:].rearrange(order, c=GROUP, h=HEADS),
-                in1=by_sin[:].rearrange(order, c=GROUP, h=HEADS),
+                in0=terms[:, 0],
+                in1=terms[:, 1],
                 op=ALU.add,
             )
 
-        def store_group(g):
-            if g % GROUPS_PER_STORE == GROUPS_PER_STORE - 1:
+        def store_run(run):
+            g = run[-1]
+            if g % STORE_GROUPS == STORE_GROUPS - 1:
                 b, first = divmod((g + 1) * GROUP - STORE_TILES, TILES)
                 nc.sync.dma_start(
                     out=out[b].rearrange("h (p c) d -> p h c d", c=TILES)[
                         :, :, first : first + STORE_TILES, :
                     ],
-                    in_=stage_of[g // GROUPS_PER_STORE][:],
+                    in_=stage_of[g // STORE_GROUPS][:],
                 )
 
-        for step in range(N_GROUPS + 3):
-            if step < N_GROUPS:
-                transpose_group(step)
-                regroup_group(step)
-            if step + LOADS_AHEAD < N_LOADS:
-                load_tiles(step + LOADS_AHEAD)
-            if step < GROUPS_PER_BATCH:
-                fill_tables(step)
-            if step >= 3:
-                rotate_products(step - 3)
-            if 1 <= step <= N_GROUPS:
-                quantise_group(step - 1)
-            if 2 <= step <= N_GROUPS + 1:
-                multiply_group(step - 2)
-                copy_unrotated(step - 2)
-            if step >= 3:
-                rotate_sum(step - 3)
-                store_group(step - 3)
+        runs, first = [], 0
+        for size in RUNS:
+            runs.append(list(range(first, first + size)))
+            first += size
+        n_loaded = loads_ahead
+        chunk_groups = TILES // GROUP // CHUNKS
+
+        for step in range(len(runs) + 3):
+            now = runs[step] if step < len(runs) else []
+            last = runs[step - 1] if 1 <= step <= len(runs) else []
+            older = runs[step - 2] if 2 <= step <= len(runs) + 1 else []
+            oldest = runs[step - 3] if 3 <= step else []
+            if now:
+                transpose_run(now)
+            if older:
+                copy_unrotated(older)
+            if now:
+                regroup_run(now)
+                g = now[0]
+                if g % chunk_groups == 0 and g < TILES // GROUP:
+                    fill_tables(nc.gpsimd if g else nc.vector, chunk_of(g // chunk_groups))
+            while n_loaded < len(LOADS) and sum(LOADS[: n_loaded - X_BUFS + 1]) <= (now[-1] + 1) * GROUP:
+                load_tiles(n_loaded)
+                n_loaded += 1
+            if last:
+                quantise_run(last)
+            if step == 1:
+                round_angles(whole2, both, other_chunks)
+                combine_angles(nc.gpsimd, turn, both, whole2, ALU.subtract, other_chunks)
+            if oldest:
+                rotate_sum(oldest)
+                store_run(oldest)
+            if older:
+                rotate_products(older)
+            if last:
+                multiply_run(last)

@@ -30,9 +30,10 @@ STORE_GROUPS = 2
 STORE_TILES = STORE_GROUPS * GROUP
 LOADS = [1, 1, 2] + [4] * 5 + [8] * 13
 LOAD_TILES = max(LOADS)
-RUNS = [1] * 4 + [2] * 12 + [1] * 4
+RUNS = [2] * 16
 
 X_BUFS = 9
+SCALAR_FINE = 5
 CHUNKS = 4
 
 ROUND = 1.5 * 2.0**23
@@ -45,9 +46,9 @@ def tile_deepseekv4attention_pb_t_kernel(tc, hidden, wq, out):
         const = ctx.enter_context(tc.tile_pool(name="const", bufs=1))
         xpool = ctx.enter_context(tc.tile_pool(name="xpool", bufs=X_BUFS))
         hpool = ctx.enter_context(tc.tile_pool(name="hpool", bufs=2))
-        gpool = ctx.enter_context(tc.tile_pool(name="gpool", bufs=3))
-        qpool = ctx.enter_context(tc.tile_pool(name="qpool", bufs=3))
-        rpool = ctx.enter_context(tc.tile_pool(name="rpool", bufs=2))
+        gpool = ctx.enter_context(tc.tile_pool(name="gpool", bufs=5))
+        qpool = ctx.enter_context(tc.tile_pool(name="qpool", bufs=5))
+        rpool = ctx.enter_context(tc.tile_pool(name="rpool", bufs=5))
         spool = ctx.enter_context(tc.tile_pool(name="spool", bufs=14))
         tpsum = ctx.enter_context(tc.psum_pool(name="tpsum", bufs=4))
         ypsum = ctx.enter_context(tc.psum_pool(name="ypsum", bufs=4))
@@ -112,12 +113,11 @@ def tile_deepseekv4attention_pb_t_kernel(tc, hidden, wq, out):
 
         for j in range(PAIRS):
             scale_position(nc.vector, coarse, j, frequency(j)[0])
-        for j in range(0, 4):
-            nc.scalar.mul(out=fine[:, j, :], in_=position[:], mul=frequency(j)[1])
-        for j in range(4, 10):
-            scale_position(nc.gpsimd, fine, j, frequency(j)[1])
-        for j in range(10, PAIRS):
-            scale_position(nc.vector, fine, j, frequency(j)[1])
+        for j in range(PAIRS):
+            if j < SCALAR_FINE:
+                nc.scalar.mul(out=fine[:, j, :], in_=position[:], mul=frequency(j)[1])
+            else:
+                scale_position(nc.vector, fine, j, frequency(j)[1])
         whole = const.tile([P, PAIRS, TILES], F32)
         part = const.tile([P, PAIRS, TILES], F32)
         both = const.tile([P, PAIRS, TILES], F32)
@@ -135,12 +135,19 @@ def tile_deepseekv4attention_pb_t_kernel(tc, hidden, wq, out):
                 op1=ALU.subtract,
             )
 
-        def combine_angles(engine, result, a, b, op, tiles):
-            engine.tensor_tensor(
-                out=result[:, :, tiles], in0=a[:, :, tiles], in1=b[:, :, tiles], op=op
+        def reduce_angles(tiles):
+            nc.vector.tensor_tensor(
+                out=part[:, :, tiles], in0=coarse[:, :, tiles], in1=whole[:, :, tiles], op=ALU.subtract
+            )
+            nc.vector.tensor_tensor(
+                out=both[:, :, tiles], in0=part[:, :, tiles], in1=fine[:, :, tiles], op=ALU.add
+            )
+            round_angles(whole2, both, tiles)
+            nc.vector.tensor_tensor(
+                out=turn[:, :, tiles], in0=both[:, :, tiles], in1=whole2[:, :, tiles], op=ALU.subtract
             )
 
-        def fill_tables(engine, tiles):
+        def fill_tables(tiles):
             n = tiles.stop - tiles.start
             half = hpool.tile([P, n, PAIRS], F32)
             square = hpool.tile([P, n, PAIRS], F32)
@@ -152,8 +159,8 @@ def tile_deepseekv4attention_pb_t_kernel(tc, hidden, wq, out):
             nc.scalar.activation(
                 out=tables[:, tiles, 1, 0, :], in_=turns, func=ACT.Sin, scale=-2.0 * math.pi
             )
-            engine.tensor_tensor(out=square[:], in0=half[:], in1=half[:], op=ALU.mult)
-            engine.tensor_scalar(
+            nc.gpsimd.tensor_tensor(out=square[:], in0=half[:], in1=half[:], op=ALU.mult)
+            nc.gpsimd.tensor_scalar(
                 out=tables[:, tiles].rearrange("p c i e j -> p c (i e) j")[:, :, 0:4:3, :],
                 in0=square[:].unsqueeze(2).to_broadcast([P, n, 2, PAIRS]),
                 scalar1=-2.0,
@@ -165,14 +172,8 @@ def tile_deepseekv4attention_pb_t_kernel(tc, hidden, wq, out):
         def chunk_of(key):
             return slice(key * TILES // CHUNKS, (key + 1) * TILES // CHUNKS)
 
-        first_chunk, other_chunks = chunk_of(0), slice(TILES // CHUNKS, TILES)
         round_angles(whole, coarse, slice(0, TILES))
-        combine_angles(nc.gpsimd, part, coarse, whole, ALU.subtract, other_chunks)
-        combine_angles(nc.gpsimd, both, part, fine, ALU.add, other_chunks)
-        combine_angles(nc.vector, part, coarse, whole, ALU.subtract, first_chunk)
-        combine_angles(nc.vector, both, part, fine, ALU.add, first_chunk)
-        round_angles(whole2, both, first_chunk)
-        combine_angles(nc.vector, turn, both, whole2, ALU.subtract, first_chunk)
+        reduce_angles(chunk_of(0))
 
         w_grouped = const.tile([P, FEATURES, 4], BF16, align_bytes=64)
         w_parts = w_grouped[:].rearrange("p (i s n) t -> p i s n t", i=2, s=2)
@@ -193,97 +194,90 @@ def tile_deepseekv4attention_pb_t_kernel(tc, hidden, wq, out):
 
         xt_of, grouped_of, codes_of, scales_of, y_of, stage_of, products_of = {}, {}, {}, {}, {}, {}, {}
 
-        def transpose_run(run):
-            for g in run:
-                for half in range(2):
-                    xt = tpsum.tile([P, 2, 2, P], F32)
-                    for i in range(2):
-                        x_sb, place = x_of[g * GROUP + 2 * half + i]
-                        x_words = x_sb[:].bitcast(F32)
-                        for u in range(2):
-                            nc.tensor.transpose(
-                                xt[:, i, u, :],
-                                x_words[:, place * WORDS + u : (place + 1) * WORDS : 2],
-                                ident[:],
-                            )
-                    xt_of[g, half] = xt
+        def transpose_group(g):
+            for half in range(2):
+                xt = tpsum.tile([P, 2, 2, P], F32)
+                for i in range(2):
+                    x_sb, place = x_of[g * GROUP + 2 * half + i]
+                    x_words = x_sb[:].bitcast(F32)
+                    for u in range(2):
+                        nc.tensor.transpose(
+                            xt[:, i, u, :],
+                            x_words[:, place * WORDS + u : (place + 1) * WORDS : 2],
+                            ident[:],
+                        )
+                xt_of[g, half] = xt
 
-        def regroup_run(run):
-            grouped = gpool.tile([P, len(run) * GROUP * HID], BF16, align_bytes=64)
+        def regroup_group(g):
+            grouped = gpool.tile([P, GROUP * HID], BF16, align_bytes=64)
             grouped_words = grouped[:].bitcast(F32).rearrange(
-                "p (half i r u) -> p half i r u", i=2, r=P, u=2
+                "p (half i r u) -> p half i r u", half=2, i=2, u=2
             )
-            for n, g in enumerate(run):
-                for half in range(2):
-                    nc.scalar.copy(
-                        out=grouped_words[:, 2 * n + half],
-                        in_=xt_of[g, half][:].rearrange("p i u r -> p i r u"),
-                    )
-            grouped_of[run[0]] = grouped
-
-        def quantise_run(run):
-            codes = qpool.tile([P, len(run) * GROUP * P], U32, align_bytes=64)
-            scales = qpool.tile([P, len(run) * GROUP * P], U8, align_bytes=64)
-            nc.vector.quantize_mx(
-                out=codes[:].bitcast(FP8X4), scales=scales[:], in_=grouped_of[run[0]][:]
-            )
-            codes_of[run[0]] = codes
-            scales_of[run[0]] = scales
-
-        def multiply_run(run):
-            codes, scales = codes_of[run[0]], scales_of[run[0]]
-            for n, g in enumerate(run):
-                y = ypsum.tile([P, GROUP, FEATURES], F32)
-                for i in range(GROUP):
-                    tokens = slice((n * GROUP + i) * P, (n * GROUP + i + 1) * P)
-                    nc.tensor.matmul_mx(
-                        out=y[:, i, :],
-                        lhsT=codes[:, tokens].bitcast(FP8X4),
-                        lhsT_scale=scales[:, tokens],
-                        rhs=w_codes[:].bitcast(FP8X4),
-                        rhs_scale=w_scales[:],
-                        start=True,
-                        stop=True,
-                    )
-                y_of[g] = y
-
-        def stage_part(run, features):
-            first = (run[0] % STORE_GROUPS) * GROUP
-            tiles = slice(first, first + len(run) * GROUP)
-            return stage_of[run[0] // STORE_GROUPS][:, :, tiles, features]
-
-        def copy_unrotated(run):
-            if run[0] % STORE_GROUPS == 0:
-                stage = spool.tile([P, HEADS, STORE_TILES, HEAD_DIM], F32)
-                stage_of[run[0] // STORE_GROUPS] = stage
-            for g in run:
+            for half in range(2):
                 nc.scalar.copy(
-                    out=stage_part([g], slice(0, NOPE_DIM)).rearrange("p h c d -> p c h d"),
-                    in_=y_of[g][:].rearrange("p c (h s d) -> p c h s d", h=HEADS, s=2)[:, :, :, 1],
+                    out=grouped_words[:, half],
+                    in_=xt_of[g, half][:].rearrange("p i u r -> p i r u"),
                 )
+            grouped_of[g] = grouped
 
-        def rotate_products(run):
-            products = rpool.tile([P, len(run), GROUP * 2, 2, HEADS, PAIRS], F32)
+        def quantise_group(g):
+            codes = qpool.tile([P, GROUP * P], U32, align_bytes=64)
+            scales = qpool.tile([P, GROUP * P], U8, align_bytes=64)
+            nc.vector.quantize_mx(
+                out=codes[:].bitcast(FP8X4), scales=scales[:], in_=grouped_of[g][:]
+            )
+            codes_of[g] = codes
+            scales_of[g] = scales
+
+        def multiply_group(g):
+            y = ypsum.tile([P, GROUP, FEATURES], F32)
+            for i in range(GROUP):
+                tokens = slice(i * P, (i + 1) * P)
+                nc.tensor.matmul_mx(
+                    out=y[:, i, :],
+                    lhsT=codes_of[g][:, tokens].bitcast(FP8X4),
+                    lhsT_scale=scales_of[g][:, tokens],
+                    rhs=w_codes[:].bitcast(FP8X4),
+                    rhs_scale=w_scales[:],
+                    start=True,
+                    stop=True,
+                )
+            y_of[g] = y
+
+        def stage_part(g, features):
+            first = (g % STORE_GROUPS) * GROUP
+            return stage_of[g // STORE_GROUPS][:, :, first : first + GROUP, features]
+
+        def copy_unrotated(g):
+            if g % STORE_GROUPS == 0:
+                stage = spool.tile([P, HEADS, STORE_TILES, HEAD_DIM], F32)
+                stage_of[g // STORE_GROUPS] = stage
+            nc.scalar.copy(
+                out=stage_part(g, slice(0, NOPE_DIM)).rearrange("p h c d -> p c h d"),
+                in_=y_of[g][:].rearrange("p c (h s d) -> p c h s d", h=HEADS, s=2)[:, :, :, 1],
+            )
+
+        def rotate_products(g):
+            first = g * GROUP % TILES
             shape = [P, GROUP * 2, 2, HEADS, PAIRS]
-            for n, g in enumerate(run):
-                first = g * GROUP % TILES
-                nc.vector.tensor_tensor(
-                    out=products[:, n],
-                    in0=y_of[g][:]
-                    .rearrange("p c (i s h j) -> p (c i) s h j", i=2, s=2, h=HEADS)[:, :, 0:1]
-                    .to_broadcast(shape),
-                    in1=tables[:, first : first + GROUP]
-                    .rearrange("p c i e j -> p (c i) e j")
-                    .unsqueeze(3)
-                    .to_broadcast(shape),
-                    op=ALU.mult,
-                )
-            products_of[run[0]] = products
-
-        def rotate_sum(run):
-            terms = products_of[run[0]][:].rearrange("p n (c i) e h j -> p i (n c) h j e", i=2)
+            products = rpool.tile(shape, F32)
             nc.vector.tensor_tensor(
-                out=stage_part(run, slice(NOPE_DIM, HEAD_DIM)).rearrange(
+                out=products[:],
+                in0=y_of[g][:]
+                .rearrange("p c (i s h j) -> p (c i) s h j", i=2, s=2, h=HEADS)[:, :, 0:1]
+                .to_broadcast(shape),
+                in1=tables[:, first : first + GROUP]
+                .rearrange("p c i e j -> p (c i) e j")
+                .unsqueeze(3)
+                .to_broadcast(shape),
+                op=ALU.mult,
+            )
+            products_of[g] = products
+
+        def rotate_sum(g):
+            terms = products_of[g][:].rearrange("p (c i) e h j -> p i c h j e", i=2)
+            nc.vector.tensor_tensor(
+                out=stage_part(g, slice(NOPE_DIM, HEAD_DIM)).rearrange(
                     "p h c (j e) -> p c h j e", e=2
                 ),
                 in0=terms[:, 0],
@@ -291,16 +285,13 @@ def tile_deepseekv4attention_pb_t_kernel(tc, hidden, wq, out):
                 op=ALU.add,
             )
 
-        def store_run(run):
-            g = run[-1]
-            if g % STORE_GROUPS == STORE_GROUPS - 1:
-                b, first = divmod((g + 1) * GROUP - STORE_TILES, TILES)
-                nc.sync.dma_start(
-                    out=out[b].rearrange("h (p c) d -> p h c d", c=TILES)[
-                        :, :, first : first + STORE_TILES, :
-                    ],
-                    in_=stage_of[g // STORE_GROUPS][:],
-                )
+        def store_groups(first, last):
+            b, c = divmod(first * GROUP, TILES)
+            place, size = (first % STORE_GROUPS) * GROUP, (last + 1 - first) * GROUP
+            nc.sync.dma_start(
+                out=out[b].rearrange("h (p c) d -> p h c d", c=TILES)[:, :, c : c + size, :],
+                in_=stage_of[first // STORE_GROUPS][:, :, place : place + size, :],
+            )
 
         runs, first = [], 0
         for size in RUNS:
@@ -309,32 +300,37 @@ def tile_deepseekv4attention_pb_t_kernel(tc, hidden, wq, out):
         n_loaded = loads_ahead
         chunk_groups = TILES // GROUP // CHUNKS
 
+        def run_of(step):
+            return runs[step] if 0 <= step < len(runs) else []
+
         for step in range(len(runs) + 3):
-            now = runs[step] if step < len(runs) else []
-            last = runs[step - 1] if 1 <= step <= len(runs) else []
-            older = runs[step - 2] if 2 <= step <= len(runs) + 1 else []
-            oldest = runs[step - 3] if 3 <= step else []
-            if now:
-                transpose_run(now)
-            if older:
-                copy_unrotated(older)
-            if now:
-                regroup_run(now)
-                g = now[0]
+            now, last, older, oldest = (run_of(step - back) for back in range(4))
+            for g in now:
+                transpose_group(g)
+            for g in older:
+                copy_unrotated(g)
+            for g in now:
+                regroup_group(g)
+            for g in now:
                 if g % chunk_groups == 0 and g < TILES // GROUP:
-                    fill_tables(nc.gpsimd if g else nc.vector, chunk_of(g // chunk_groups))
+                    fill_tables(chunk_of(g // chunk_groups))
             while n_loaded < len(LOADS) and sum(LOADS[: n_loaded - X_BUFS + 1]) <= (now[-1] + 1) * GROUP:
                 load_tiles(n_loaded)
                 n_loaded += 1
-            if last:
-                quantise_run(last)
-            if step == 1:
-                round_angles(whole2, both, other_chunks)
-                combine_angles(nc.gpsimd, turn, both, whole2, ALU.subtract, other_chunks)
-            if oldest:
-                rotate_sum(oldest)
-                store_run(oldest)
-            if older:
-                rotate_products(older)
-            if last:
-                multiply_run(last)
+            for g in last[-1:]:
+                quantise_group(g)
+            for g in oldest:
+                rotate_sum(g)
+                if g >= N_GROUPS - STORE_GROUPS:
+                    store_groups(g, g)
+                elif g % STORE_GROUPS == STORE_GROUPS - 1:
+                    store_groups(g - STORE_GROUPS + 1, g)
+            for g in older:
+                rotate_products(g)
+            for g in now[:-1]:
+                quantise_group(g)
+            for g in now:
+                if g % chunk_groups == 0 and g < TILES // GROUP - chunk_groups:
+                    reduce_angles(chunk_of(g // chunk_groups + 1))
+            for g in last:
+                multiply_group(g)

@@ -173,7 +173,7 @@ def tile_deepseekv4attention_pb_t_kernel(tc, hidden, wq, out):
             return slice(key * TILES // CHUNKS, (key + 1) * TILES // CHUNKS)
 
         round_angles(whole, coarse, slice(0, TILES))
-        reduce_angles(chunk_of(0))
+        reduce_angles(slice(0, TILES // 2))
 
         w_grouped = const.tile([P, FEATURES, 4], BF16, align_bytes=64)
         w_parts = w_grouped[:].rearrange("p (i s n) t -> p i s n t", i=2, s=2)
@@ -307,8 +307,6 @@ def tile_deepseekv4attention_pb_t_kernel(tc, hidden, wq, out):
             now, last, older, oldest = (run_of(step - back) for back in range(4))
             for g in now:
                 transpose_group(g)
-            for g in older:
-                copy_unrotated(g)
             for g in now:
                 regroup_group(g)
             for g in now:
@@ -317,20 +315,20 @@ def tile_deepseekv4attention_pb_t_kernel(tc, hidden, wq, out):
             while n_loaded < len(LOADS) and sum(LOADS[: n_loaded - X_BUFS + 1]) <= (now[-1] + 1) * GROUP:
                 load_tiles(n_loaded)
                 n_loaded += 1
-            for g in last[-1:]:
-                quantise_group(g)
             for g in oldest:
                 rotate_sum(g)
                 if g >= N_GROUPS - STORE_GROUPS:
                     store_groups(g, g)
                 elif g % STORE_GROUPS == STORE_GROUPS - 1:
                     store_groups(g - STORE_GROUPS + 1, g)
+            for g in last[-1:]:
+                quantise_group(g)
             for g in older:
                 rotate_products(g)
+                copy_unrotated(g)
             for g in now[:-1]:
                 quantise_group(g)
-            for g in now:
-                if g % chunk_groups == 0 and g < TILES // GROUP - chunk_groups:
-                    reduce_angles(chunk_of(g // chunk_groups + 1))
+            if step == 0:
+                reduce_angles(slice(TILES // 2, TILES))
             for g in last:
                 multiply_group(g)

@@ -26,8 +26,7 @@ TILES = SEQ // P
 ALL_TILES = BATCH * TILES
 GROUP = 4
 N_GROUPS = ALL_TILES // GROUP
-STORE_GROUPS = 2
-STORE_TILES = STORE_GROUPS * GROUP
+STORES = [16] * 6 + [8] * 3 + [4] * 2
 LOADS = [1, 1, 2] + [4] * 5 + [8] * 13
 LOAD_TILES = max(LOADS)
 RUNS = [2] * 16
@@ -49,7 +48,6 @@ def tile_deepseekv4attention_pb_t_kernel(tc, hidden, wq, out):
         gpool = ctx.enter_context(tc.tile_pool(name="gpool", bufs=5))
         qpool = ctx.enter_context(tc.tile_pool(name="qpool", bufs=5))
         rpool = ctx.enter_context(tc.tile_pool(name="rpool", bufs=5))
-        spool = ctx.enter_context(tc.tile_pool(name="spool", bufs=14))
         tpsum = ctx.enter_context(tc.psum_pool(name="tpsum", bufs=4))
         ypsum = ctx.enter_context(tc.psum_pool(name="ypsum", bufs=4))
         ctx.enter_context(tc.manual_schedule())
@@ -122,7 +120,7 @@ def tile_deepseekv4attention_pb_t_kernel(tc, hidden, wq, out):
         part = const.tile([P, PAIRS, TILES], F32)
         both = const.tile([P, PAIRS, TILES], F32)
         whole2 = const.tile([P, PAIRS, TILES], F32)
-        turn = const.tile([P, PAIRS, TILES], F32)
+        turn = const.tile([P, 2, PAIRS, TILES], F32)
         tables = const.tile([P, TILES, 2, 2, PAIRS], F32)
 
         def round_angles(rounded, angles, tiles):
@@ -144,22 +142,23 @@ def tile_deepseekv4attention_pb_t_kernel(tc, hidden, wq, out):
             )
             round_angles(whole2, both, tiles)
             nc.vector.tensor_tensor(
-                out=turn[:, :, tiles], in0=both[:, :, tiles], in1=whole2[:, :, tiles], op=ALU.subtract
+                out=turn[:, 1, :, tiles], in0=both[:, :, tiles], in1=whole2[:, :, tiles], op=ALU.subtract
+            )
+            nc.vector.tensor_scalar(
+                out=turn[:, 0, :, tiles], in0=turn[:, 1, :, tiles], scalar1=0.5, scalar2=None, op0=ALU.mult
             )
 
         def fill_tables(tiles):
             n = tiles.stop - tiles.start
-            half = hpool.tile([P, n, PAIRS], F32)
             square = hpool.tile([P, n, PAIRS], F32)
-            turns = turn[:, :, tiles].rearrange("p j c -> p c j")
-            nc.scalar.activation(out=half[:], in_=turns, func=ACT.Sin, scale=math.pi)
             nc.scalar.activation(
-                out=tables[:, tiles, 0, 1, :], in_=turns, func=ACT.Sin, scale=2.0 * math.pi
+                out=tables[:, tiles, 0],
+                in_=turn[:, :, :, tiles].rearrange("p u j c -> p c u j"),
+                func=ACT.Sin,
+                scale=2.0 * math.pi,
             )
-            nc.scalar.activation(
-                out=tables[:, tiles, 1, 0, :], in_=turns, func=ACT.Sin, scale=-2.0 * math.pi
-            )
-            nc.gpsimd.tensor_tensor(out=square[:], in0=half[:], in1=half[:], op=ALU.mult)
+            half = tables[:, tiles, 0, 0, :]
+            nc.gpsimd.tensor_tensor(out=square[:], in0=half, in1=half, op=ALU.mult)
             nc.gpsimd.tensor_scalar(
                 out=tables[:, tiles].rearrange("p c i e j -> p c (i e) j")[:, :, 0:4:3, :],
                 in0=square[:].unsqueeze(2).to_broadcast([P, n, 2, PAIRS]),
@@ -167,6 +166,15 @@ def tile_deepseekv4attention_pb_t_kernel(tc, hidden, wq, out):
                 scalar2=1.0,
                 op0=ALU.mult,
                 op1=ALU.add,
+            )
+
+        def fill_negative_sines(tiles):
+            nc.vector.tensor_scalar(
+                out=tables[:, tiles, 1, 0, :],
+                in0=tables[:, tiles, 0, 1, :],
+                scalar1=-1.0,
+                scalar2=None,
+                op0=ALU.mult,
             )
 
         def chunk_of(key):
@@ -192,7 +200,7 @@ def tile_deepseekv4attention_pb_t_kernel(tc, hidden, wq, out):
             in_=w_grouped[:].rearrange("p n t -> p (n t)"),
         )
 
-        xt_of, grouped_of, codes_of, scales_of, y_of, stage_of, products_of = {}, {}, {}, {}, {}, {}, {}
+        xt_of, grouped_of, codes_of, scales_of, y_of, products_of = {}, {}, {}, {}, {}, {}
 
         def transpose_group(g):
             for half in range(2):
@@ -244,14 +252,13 @@ def tile_deepseekv4attention_pb_t_kernel(tc, hidden, wq, out):
                 )
             y_of[g] = y
 
+        stages = [const.tile([P, HEADS, TILES, HEAD_DIM], F32, name="stage%d" % b) for b in range(BATCH)]
+
         def stage_part(g, features):
-            first = (g % STORE_GROUPS) * GROUP
-            return stage_of[g // STORE_GROUPS][:, :, first : first + GROUP, features]
+            b, c = divmod(g * GROUP, TILES)
+            return stages[b][:, :, c : c + GROUP, features]
 
         def copy_unrotated(g):
-            if g % STORE_GROUPS == 0:
-                stage = spool.tile([P, HEADS, STORE_TILES, HEAD_DIM], F32)
-                stage_of[g // STORE_GROUPS] = stage
             nc.scalar.copy(
                 out=stage_part(g, slice(0, NOPE_DIM)).rearrange("p h c d -> p c h d"),
                 in_=y_of[g][:].rearrange("p c (h s d) -> p c h s d", h=HEADS, s=2)[:, :, :, 1],
@@ -285,13 +292,20 @@ def tile_deepseekv4attention_pb_t_kernel(tc, hidden, wq, out):
                 op=ALU.add,
             )
 
-        def store_groups(first, last):
-            b, c = divmod(first * GROUP, TILES)
-            place, size = (first % STORE_GROUPS) * GROUP, (last + 1 - first) * GROUP
-            nc.sync.dma_start(
-                out=out[b].rearrange("h (p c) d -> p h c d", c=TILES)[:, :, c : c + size, :],
-                in_=stage_of[first // STORE_GROUPS][:, :, place : place + size, :],
-            )
+        store_of = {}
+        first = 0
+        for size in STORES:
+            store_of[(first + size) // GROUP - 1] = (first, size)
+            first += size
+
+        def store_after(g):
+            if g in store_of:
+                first, size = store_of[g]
+                b, c = divmod(first, TILES)
+                nc.sync.dma_start(
+                    out=out[b].rearrange("h (p c) d -> p h c d", c=TILES)[:, :, c : c + size, :],
+                    in_=stages[b][:, :, c : c + size, :],
+                )
 
         runs, first = [], 0
         for size in RUNS:
@@ -317,12 +331,12 @@ def tile_deepseekv4attention_pb_t_kernel(tc, hidden, wq, out):
                 n_loaded += 1
             for g in oldest:
                 rotate_sum(g)
-                if g >= N_GROUPS - STORE_GROUPS:
-                    store_groups(g, g)
-                elif g % STORE_GROUPS == STORE_GROUPS - 1:
-                    store_groups(g - STORE_GROUPS + 1, g)
+                store_after(g)
             for g in last[-1:]:
                 quantise_group(g)
+            for g in last:
+                if g % chunk_groups == 0 and g < TILES // GROUP:
+                    fill_negative_sines(chunk_of(g // chunk_groups))
             for g in older:
                 rotate_products(g)
                 copy_unrotated(g)

import math
from contextlib import ExitStack

import concourse.mybir as mybir
from concourse.masks import make_identity

F32 = mybir.dt.float32
BF16 = mybir.dt.bfloat16
U32 = mybir.dt.uint32
U8 = mybir.dt.uint8
FP8X4 = mybir.dt.float8_e4m3fn_x4
ALU = mybir.AluOpType
ACT = mybir.ActivationFunctionType

P = 128
BATCH, SEQ, HID = 4, 4096, 512
HEADS, HEAD_DIM, ROPE_DIM = 2, 64, 32
NOPE_DIM = HEAD_DIM - ROPE_DIM
PAIRS = ROPE_DIM // 2
FEATURES = HEADS * HEAD_DIM
THETA = 10000.0
FLOPS = 2 * BATCH * SEQ * HID * FEATURES

WORDS = HID // 2
TILES = SEQ // P
ALL_TILES = BATCH * TILES
GROUP = 4
N_GROUPS = ALL_TILES // GROUP
STORES = [16] * 6 + [8] * 3 + [4] * 2
LOADS = [1, 1, 2] + [4] * 5 + [8] * 13
LOAD_TILES = max(LOADS)
RUNS = [2] * 16

X_BUFS = 9
SCALAR_FINE = 5
CHUNKS = 4

ROUND = 1.5 * 2.0**23
COARSE = 2.0**14


def tile_deepseekv4attention_pb_t_kernel(tc, hidden, wq, out):
    nc = tc.nc
    with ExitStack() as ctx:
        const = ctx.enter_context(tc.tile_pool(name="const", bufs=1))
        xpool = ctx.enter_context(tc.tile_pool(name="xpool", bufs=X_BUFS))
        hpool = ctx.enter_context(tc.tile_pool(name="hpool", bufs=2))
        gpool = ctx.enter_context(tc.tile_pool(name="gpool", bufs=5))
        qpool = ctx.enter_context(tc.tile_pool(name="qpool", bufs=5))
        rpool = ctx.enter_context(tc.tile_pool(name="rpool", bufs=5))
        tpsum = ctx.enter_context(tc.psum_pool(name="tpsum", bufs=4))
        ypsum = ctx.enter_context(tc.psum_pool(name="ypsum", bufs=4))
        ctx.enter_context(tc.manual_schedule())

        x_of = {}

        def load_tiles(n):
            size, first = LOADS[n], sum(LOADS[:n])
            b, c = divmod(first, TILES)
            if size == LOAD_TILES:
                x_sb = xpool.tile([P, size * HID], BF16)
            else:
                x_sb = const.tile([P, size * HID], BF16, name="x%d" % n)
            nc.sync.dma_start(
                out=x_sb[:],
                in_=hidden[b].rearrange("(p c) k -> p (c k)", c=TILES)[:, c * HID : (c + size) * HID],
            )
            for i in range(size):
                x_of[first + i] = (x_sb, i)

        loads_ahead = LOADS.index(LOAD_TILES) + X_BUFS
        for n in range(loads_ahead):
            load_tiles(n)

        w_raw = const.tile([P, 4, FEATURES], BF16)
        nc.scalar.dma_start(out=w_raw[:], in_=wq.rearrange("(p t) n -> p t n", t=4))

        position = const.tile([P, TILES], F32)
        nc.gpsimd.iota(
            position[:],
            pattern=[[1, TILES]],
            base=0,
            channel_multiplier=TILES,
            allow_small_or_imprecise_dtypes=True,
        )
        ident = const.tile([P, P], F32)
        make_identity(nc, ident[:])

        zero = const.tile([P, 1], F32)
        nc.vector.memset(zero[:], 0.0)
        warm = const.tile([P, 1], F32)
        nc.scalar.activation(out=warm[:], in_=zero[:], func=ACT.Sin)

        coarse = const.tile([P, PAIRS, TILES], F32)
        fine = const.tile([P, PAIRS, TILES], F32)

        def frequency(j):
            turns = THETA ** (-j / PAIRS) / (2.0 * math.pi)
            turns_coarse = round(turns * COARSE) / COARSE
            return turns_coarse, turns - turns_coarse

        def scale_position(engine, angle, j, factor):
            engine.tensor_scalar(
                out=angle[:, j, :],
                in0=position[:],
                scalar1=factor,
                scalar2=0.0,
                op0=ALU.mult,
                op1=ALU.add,
            )

        for j in range(PAIRS):
            scale_position(nc.vector, coarse, j, frequency(j)[0])
        for j in range(PAIRS):
            if j < SCALAR_FINE:
                nc.scalar.mul(out=fine[:, j, :], in_=position[:], mul=frequency(j)[1])
            else:
                scale_position(nc.vector, fine, j, frequency(j)[1])
        whole = const.tile([P, PAIRS, TILES], F32)
        part = const.tile([P, PAIRS, TILES], F32)
        both = const.tile([P, PAIRS, TILES], F32)
        whole2 = const.tile([P, PAIRS, TILES], F32)
        turn = const.tile([P, 2, PAIRS, TILES], F32)
        tables = const.tile([P, TILES, 2, 2, PAIRS], F32)

        def round_angles(rounded, angles, tiles):
            nc.vector.tensor_scalar(
                out=rounded[:, :, tiles],
                in0=angles[:, :, tiles],
                scalar1=ROUND,
                scalar2=ROUND,
                op0=ALU.add,
                op1=ALU.subtract,
            )

        def reduce_angles(tiles):
            nc.vector.tensor_tensor(
                out=part[:, :, tiles], in0=coarse[:, :, tiles], in1=whole[:, :, tiles], op=ALU.subtract
            )
            nc.vector.tensor_tensor(
                out=both[:, :, tiles], in0=part[:, :, tiles], in1=fine[:, :, tiles], op=ALU.add
            )
            round_angles(whole2, both, tiles)
            nc.vector.tensor_tensor(
                out=turn[:, 1, :, tiles], in0=both[:, :, tiles], in1=whole2[:, :, tiles], op=ALU.subtract
            )
            nc.vector.tensor_scalar(
                out=turn[:, 0, :, tiles], in0=turn[:, 1, :, tiles], scalar1=0.5, scalar2=None, op0=ALU.mult
            )

        def fill_tables(tiles):
            n = tiles.stop - tiles.start
            square = hpool.tile([P, n, PAIRS], F32)
            nc.scalar.activation(
                out=tables[:, tiles, 0],
                in_=turn[:, :, :, tiles].rearrange("p u j c -> p c u j"),
                func=ACT.Sin,
                scale=2.0 * math.pi,
            )
            half = tables[:, tiles, 0, 0, :]
            nc.gpsimd.tensor_tensor(out=square[:], in0=half, in1=half, op=ALU.mult)
            nc.gpsimd.tensor_scalar(
                out=tables[:, tiles].rearrange("p c i e j -> p c (i e) j")[:, :, 0:4:3, :],
                in0=square[:].unsqueeze(2).to_broadcast([P, n, 2, PAIRS]),
                scalar1=-2.0,
                scalar2=1.0,
                op0=ALU.mult,
                op1=ALU.add,
            )

        def fill_negative_sines(tiles):
            nc.vector.tensor_scalar(
                out=tables[:, tiles, 1, 0, :],
                in0=tables[:, tiles, 0, 1, :],
                scalar1=-1.0,
                scalar2=None,
                op0=ALU.mult,
            )

        def chunk_of(key):
            return slice(key * TILES // CHUNKS, (key + 1) * TILES // CHUNKS)

        round_angles(whole, coarse, slice(0, TILES))
        reduce_angles(slice(0, TILES // 2))

        w_grouped = const.tile([P, FEATURES, 4], BF16, align_bytes=64)
        w_parts = w_grouped[:].rearrange("p (i s n) t -> p i s n t", i=2, s=2)
        by_head = w_raw[:].rearrange("p t (h d) -> p h d t", h=HEADS)
        nc.scalar.copy(out=w_parts[:, :, 1], in_=by_head[:, :, 0:NOPE_DIM, :])
        by_pair = by_head[:, :, NOPE_DIM:HEAD_DIM, :].rearrange("p h (j e) t -> p e h j t", e=2)
        for e in range(2):
            nc.vector.tensor_copy(
                out=w_parts[:, e, 0].rearrange("p (h j) t -> p h j t", h=HEADS), in_=by_pair[:, e]
            )
        w_codes = const.tile([P, FEATURES], U32, align_bytes=64)
        w_scales = const.tile([P, FEATURES], U8, align_bytes=64)
        nc.vector.quantize_mx(
            out=w_codes[:].bitcast(FP8X4),
            scales=w_scales[:],
            in_=w_grouped[:].rearrange("p n t -> p (n t)"),
        )

        xt_of, grouped_of, codes_of, scales_of, y_of, products_of = {}, {}, {}, {}, {}, {}

        def transpose_group(g):
            for half in range(2):
                xt = tpsum.tile([P, 2, 2, P], F32)
                for i in range(2):
                    x_sb, place = x_of[g * GROUP + 2 * half + i]
                    x_words = x_sb[:].bitcast(F32)
                    for u in range(2):
                        nc.tensor.transpose(
                            xt[:, i, u, :],
                            x_words[:, place * WORDS + u : (place + 1) * WORDS : 2],
                            ident[:],
                        )
                xt_of[g, half] = xt

        def regroup_group(g):
            grouped = gpool.tile([P, GROUP * HID], BF16, align_bytes=64)
            grouped_words = grouped[:].bitcast(F32).rearrange(
                "p (half i r u) -> p half i r u", half=2, i=2, u=2
            )
            for half in range(2):
                nc.scalar.copy(
                    out=grouped_words[:, half],
                    in_=xt_of[g, half][:].rearrange("p i u r -> p i r u"),
                )
            grouped_of[g] = grouped

        def quantise_group(g):
            codes = qpool.tile([P, GROUP * P], U32, align_bytes=64)
            scales = qpool.tile([P, GROUP * P], U8, align_bytes=64)
            nc.vector.quantize_mx(
                out=codes[:].bitcast(FP8X4), scales=scales[:], in_=grouped_of[g][:]
            )
            codes_of[g] = codes
            scales_of[g] = scales

        def multiply_group(g):
            y = ypsum.tile([P, GROUP, FEATURES], F32)
            for i in range(GROUP):
                tokens = slice(i * P, (i + 1) * P)
                nc.tensor.matmul_mx(
                    out=y[:, i, :],
                    lhsT=codes_of[g][:, tokens].bitcast(FP8X4),
                    lhsT_scale=scales_of[g][:, tokens],
                    rhs=w_codes[:].bitcast(FP8X4),
                    rhs_scale=w_scales[:],
                    start=True,
                    stop=True,
                )
            y_of[g] = y

        stages = [const.tile([P, HEADS, TILES, HEAD_DIM], F32, name="stage%d" % b) for b in range(BATCH)]

        def stage_part(g, features):
            b, c = divmod(g * GROUP, TILES)
            return stages[b][:, :, c : c + GROUP, features]

        def copy_unrotated(g):
            nc.scalar.copy(
                out=stage_part(g, slice(0, NOPE_DIM)).rearrange("p h c d -> p c h d"),
                in_=y_of[g][:].rearrange("p c (h s d) -> p c h s d", h=HEADS, s=2)[:, :, :, 1],
            )

        def rotate_products(g):
            first = g * GROUP % TILES
            shape = [P, GROUP * 2, 2, HEADS, PAIRS]
            products = rpool.tile(shape, F32)
            nc.vector.tensor_tensor(
                out=products[:],
                in0=y_of[g][:]
                .rearrange("p c (i s h j) -> p (c i) s h j", i=2, s=2, h=HEADS)[:, :, 0:1]
                .to_broadcast(shape),
                in1=tables[:, first : first + GROUP]
                .rearrange("p c i e j -> p (c i) e j")
                .unsqueeze(3)
                .to_broadcast(shape),
                op=ALU.mult,
            )
            products_of[g] = products

        def rotate_sum(g):
            terms = products_of[g][:].rearrange("p (c i) e h j -> p i c h j e", i=2)
            nc.vector.tensor_tensor(
                out=stage_part(g, slice(NOPE_DIM, HEAD_DIM)).rearrange(
                    "p h c (j e) -> p c h j e", e=2
                ),
                in0=terms[:, 0],
                in1=terms[:, 1],
                op=ALU.add,
            )

        store_of = {}
        first = 0
        for size in STORES:
            store_of[(first + size) // GROUP - 1] = (first, size)
            first += size

        def store_after(g):
            if g in store_of:
                first, size = store_of[g]
                b, c = divmod(first, TILES)
                nc.sync.dma_start(
                    out=out[b].rearrange("h (p c) d -> p h c d", c=TILES)[:, :, c : c + size, :],
                    in_=stages[b][:, :, c : c + size, :],
                )

        runs, first = [], 0
        for size in RUNS:
            runs.append(list(range(first, first + size)))
            first += size
        n_loaded = loads_ahead
        chunk_groups = TILES // GROUP // CHUNKS

        def run_of(step):
            return runs[step] if 0 <= step < len(runs) else []

        for step in range(len(runs) + 3):
            now, last, older, oldest = (run_of(step - back) for back in range(4))
            for g in now:
                transpose_group(g)
            for g in now:
                regroup_group(g)
            for g in now:
                if g % chunk_groups == 0 and g < TILES // GROUP:
                    fill_tables(chunk_of(g // chunk_groups))
            while n_loaded < len(LOADS) and sum(LOADS[: n_loaded - X_BUFS + 1]) <= (now[-1] + 1) * GROUP:
                load_tiles(n_loaded)
                n_loaded += 1
            for g in oldest:
                rotate_sum(g)
                store_after(g)
            for g in last[-1:]:
                quantise_group(g)
            for g in last:
                if g % chunk_groups == 0 and g < TILES // GROUP:
                    fill_negative_sines(chunk_of(g // chunk_groups))
            for g in older:
                rotate_products(g)
                copy_unrotated(g)
            for g in now[:-1]:
                quantise_group(g)
            if step == 0:
                reduce_angles(slice(TILES // 2, TILES))
            for g in last:
                multiply_group(g)
